import numpy as np
import ml_dtypes


def mxq(x, axis, fmt="e4m3"):
    dtype, down = {"e4m3": (ml_dtypes.float8_e4m3fn, 7), "e5m2": (ml_dtypes.float8_e5m2, 14)}[fmt]
    v = np.moveaxis(np.asarray(x, np.float32).astype(ml_dtypes.bfloat16).astype(np.float64), axis, -1)
    blocks = v.reshape(v.shape[:-1] + (-1, 32))
    amax = np.abs(blocks).max(-1, keepdims=True)
    byte = np.maximum(np.where(amax > 0, np.frexp(amax)[1] - 1 + 127, 0) - down, 1)
    scale = np.exp2(byte - 127.0)
    codes = (blocks / scale).astype(np.float32).astype(dtype).astype(np.float64)
    return np.moveaxis((codes * scale).reshape(v.shape), -1, axis)


WIDE = False


def mx_kscale(k):
    if not WIDE:
        return np.ones(k)
    levels = np.array([10, -10, 5, -5, 0])
    a = np.random.permutation(np.resize(levels, k // 512 * 4)).reshape(k // 512, 4)
    idx = np.arange(k)
    return np.exp2(a[idx // 512, idx % 128 // 32])


BF16 = ml_dtypes.bfloat16


def bf(x):
    return np.asarray(x, np.float32).astype(BF16)


def f64(x):
    return np.asarray(x).astype(np.float64)


E2M1 = np.array([0.0, 0.5, 1.0, 1.5, 2.0, 3.0, 4.0, 6.0, -0.0, -0.5, -1.0, -1.5, -2.0, -3.0, -4.0, -6.0])


def pack_weight(w, fmt):
    k, n = w.shape
    w = f64(bf(w)).reshape(k // 32, 32, n)
    amax = np.abs(w).max(1)
    if fmt == "e4m3":
        byte = np.frexp(amax)[1] - 1 + 127 - 7
    else:
        mant, ex = np.frexp(amax / 6.0)
        byte = np.where(mant > 0.5, ex, ex - 1) + 127
    byte = np.clip(np.where(amax > 0, byte, 1), 1, 254)
    scaled = (w * np.exp2(127.0 - byte)[:, None, :]).reshape(k, n).astype(np.float32)
    by_word = np.ascontiguousarray(scaled.reshape(k // 512, 128, 4, n).transpose(0, 1, 3, 2))
    if fmt == "e4m3":
        words = by_word.astype(ml_dtypes.float8_e4m3fn).view(np.uint8)
    else:
        c = by_word.astype(ml_dtypes.float4_e2m1fn).view(np.uint8) & 0xF
        words = c[..., 0::2] | (c[..., 1::2] << 4)
    return np.ascontiguousarray(words), np.ascontiguousarray(byte.astype(np.uint8).reshape(k // 512, 16, n))


def unpack_weight(words, scales, fmt):
    g, p, n, _ = words.shape
    if fmt == "e4m3":
        vals = np.ascontiguousarray(words).view(ml_dtypes.float8_e4m3fn).astype(np.float64)
    else:
        nib = np.empty((g, p, n, 4), np.uint8)
        nib[..., 0::2] = words & 0xF
        nib[..., 1::2] = words >> 4
        vals = E2M1[nib]
    vals = vals * np.repeat(np.exp2(scales.astype(np.float64) - 127.0), 8, axis=1)[..., None]
    return vals.transpose(0, 1, 3, 2).reshape(g * 512, n)


B, N, C, D = 2, 128, 2048, 2048
ETA, TAU = 1.0, 1.5
FMT = "e4m3"


def setup_inputs():
    s, t = mx_kscale(C), mx_kscale(D)
    a = 2.0 * (C / D) ** 0.25 / np.sqrt(C)
    H_t = bf(np.random.standard_normal((B, N, C)) * s)
    A_stat = bf(np.random.random((N, N)))
    M_mask = bf(np.random.random((N, N)) - 0.25)
    Wq = np.random.standard_normal((D, C)) * a * t[:, None] / s
    Wk = np.random.standard_normal((D, C)) * a / t[:, None] / s
    Wq_words, Wq_scales = pack_weight(np.ascontiguousarray(Wq.T), FMT)
    Wk_words, Wk_scales = pack_weight(np.ascontiguousarray(Wk.T), FMT)
    return {"H_t": H_t,
            "A_stat": A_stat,
            "M_mask": M_mask,
            "Wq_words": Wq_words,
            "Wq_scales": Wq_scales,
            "Wk_words": Wk_words,
            "Wk_scales": Wk_scales}


def reference(H_t, A_stat, M_mask, Wq_words, Wq_scales, Wk_words, Wk_scales):
    c = H_t.shape[-1]
    hq = mxq(f64(H_t), 2, "e4m3")
    Q = hq @ unpack_weight(Wq_words, Wq_scales, FMT)
    K = hq @ unpack_weight(Wk_words, Wk_scales, FMT)
    logits = (mxq(Q, 2, "e4m3") @ mxq(K, 2, "e4m3").transpose(0, 2, 1)) / (np.sqrt(c) * TAU)
    logits = 0.5 * (logits + logits.transpose(0, 2, 1))
    n = logits.shape[-1]
    eye = np.eye(n, dtype=bool)
    logits = np.where(eye[None, :, :], -np.inf, logits)
    A_bias = np.where(eye, 0.0, f64(A_stat))
    logits = logits + ETA * A_bias[None, :, :]
    logits = np.where((f64(M_mask) <= 0)[None, :, :], -np.inf, logits)
    e = np.exp(logits - logits.max(-1, keepdims=True))
    return e / e.sum(-1, keepdims=True)

@@ -1,0 +1,194 @@
+from contextlib import ExitStack
+import math
+
+import concourse.bass as bass
+import concourse.mybir as mybir
+import concourse.tile as tile
+from concourse.masks import make_identity
+
+F32 = mybir.dt.float32
+BF16 = mybir.dt.bfloat16
+I32 = mybir.dt.int32
+U32 = mybir.dt.uint32
+U8 = mybir.dt.uint8
+FP8X4 = mybir.dt.float8_e4m3fn_x4
+ALU = mybir.AluOpType
+ACT = mybir.ActivationFunctionType
+
+P = 128
+B = 2
+C = 2048
+D = 2048
+TOK = B * P
+KG = C // 512
+DG = D // 512
+TAU = 1.5
+BIG = 1.0e30
+
+FLOPS = 2 * 2 * B * P * C * D + 2 * B * P * P * D
+
+
+def tile_dynamicgraphattention_w_kernel(
+    tc, H_t, A_stat, M_mask, Wq_words, Wq_scales, Wk_words, Wk_scales, out
+):
+    nc = tc.nc
+    words = (Wq_words, Wk_words)
+    scales = (Wq_scales, Wk_scales)
+    with ExitStack() as ctx:
+        keep = ctx.enter_context(tc.tile_pool(name="keep", bufs=1))
+        ring = ctx.enter_context(tc.tile_pool(name="ring", bufs=4))
+        banks = ctx.enter_context(tc.psum_pool(name="banks", bufs=6))
+        lgp = ctx.enter_context(tc.psum_pool(name="lgp", bufs=1))
+        ctx.enter_context(tc.manual_schedule())
+
+        planes = keep.tile([P, 2 * D], U8, align_bytes=64, name="planes")
+        h_sb = [keep.tile([P, C], BF16, name="h_sb%d" % b) for b in range(B)]
+        w_sb = [keep.tile([P, KG, 512], U32, align_bytes=64, name="w_sb%d" % c) for c in range(2 * DG)]
+        a_bf = keep.tile([P, P], BF16, name="a_bf")
+        m_bf = keep.tile([P, P], BF16, name="m_bf")
+        ident = keep.tile([P, P], F32, name="ident")
+        warm = keep.tile([P, 1], F32, name="warm")
+        warm2 = keep.tile([P, 1], F32, name="warm2")
+
+        nc.vector.memset(planes[:].bitcast(I32), 0)
+        nc.vector.memset(warm[:], 0.0)
+        nc.scalar.activation(out=warm2[:], in_=warm[:], func=ACT.Exp)
+        make_identity(nc, ident[:])
+        nc.gpsimd.dma_start(out=a_bf[:], in_=A_stat)
+        nc.gpsimd.dma_start(out=m_bf[:], in_=M_mask)
+
+        def load_scales(x):
+            for q in range(4):
+                nc.sync.dma_start(
+                    out=planes[32 * q : 32 * q + 16, D * x : D * (x + 1)].bitcast(I32),
+                    in_=scales[x][:, 4 * q : 4 * q + 4, :].bitcast(I32),
+                )
+
+        def load_words(c):
+            x, grp = c % 2, c // 2
+            src = words[x].rearrange("g p n t -> p g (n t)")
+            nc.sync.dma_start(
+                out=w_sb[c][:].bitcast(I32),
+                in_=src[:, :, 2048 * grp : 2048 * (grp + 1)].bitcast(I32),
+            )
+
+        for b in range(B):
+            nc.sync.dma_start(out=h_sb[b][:], in_=H_t[b])
+        load_scales(0)
+        load_words(0)
+        load_scales(1)
+        for c in range(1, 2 * DG):
+            load_words(c)
+
+        h_words = keep.tile([P, KG, TOK], U32, align_bytes=64, name="h_words")
+        h_scale = keep.tile([P, KG, TOK], U8, align_bytes=64, name="h_scale")
+        h_grp = [keep.tile([P, 4 * TOK], BF16, align_bytes=64, name="h_grp%d" % g) for g in range(KG)]
+        xt = [banks.tile([P, 2, TOK], F32, tag="bank", name="xt%d" % g) for g in range(KG)]
+        for b in range(B):
+            hw32 = h_sb[b][:].bitcast(F32)
+            for g in range(KG):
+                for u in range(2):
+                    nc.tensor.transpose(
+                        xt[g][:, u, P * b : P * (b + 1)],
+                        hw32[:, 256 * g + u : 256 * (g + 1) : 2],
+                        ident[:],
+                    )
+        for g in (0, 2, 1, 3):
+            dst = h_grp[g][:].bitcast(F32).rearrange("p (w u) -> p w u", u=2)
+            src = xt[g][:].rearrange("p u w -> p w u")
+            if g % 2 == 0:
+                nc.vector.tensor_copy(out=dst, in_=src)
+            else:
+                nc.scalar.copy(out=dst, in_=src)
+        for g in range(KG):
+            nc.vector.quantize_mx(
+                out=h_words[:, g, :].bitcast(FP8X4), scales=h_scale[:, g, :], in_=h_grp[g][:]
+            )
+
+        not_i = keep.tile([P, P], F32, name="not_i")
+        allowed = keep.tile([P, P], F32, name="allowed")
+        a_keep = keep.tile([P, P], F32, name="a_keep")
+        neg_b = keep.tile([P, P], F32, name="neg_b")
+        nc.vector.tensor_scalar(out=not_i[:], in0=ident[:], scalar1=-1.0, scalar2=1.0, op0=ALU.mult, op1=ALU.add)
+        nc.vector.scalar_tensor_tensor(
+            out=allowed[:], in0=m_bf[:], scalar=0.0, in1=not_i[:], op0=ALU.is_gt, op1=ALU.mult
+        )
+        nc.vector.tensor_tensor(out=a_keep[:], in0=a_bf[:], in1=allowed[:], op=ALU.mult)
+        nc.vector.tensor_scalar(out=neg_b[:], in0=allowed[:], scalar1=-BIG, scalar2=BIG, op0=ALU.mult, op1=ALU.add)
+        nc.vector.tensor_tensor(out=neg_b[:], in0=neg_b[:], in1=a_keep[:], op=ALU.subtract)
+
+        x_words = [keep.tile([P, TOK], U32, align_bytes=64, name="x_words%d" % c) for c in range(2 * DG)]
+        x_scale = [keep.tile([P, TOK], U8, align_bytes=64, name="x_scale%d" % c) for c in range(2 * DG)]
+        lg = [lgp.tile([P, P], F32, name="lg%d" % b) for b in range(B)]
+
+        def project(c):
+            x, grp = c % 2, c // 2
+            grouped = ring.tile([P, 4 * TOK], BF16, align_bytes=64, tag="grouped", name="grouped%d" % c)
+            gview = grouped[:].rearrange("p (w t) -> p w t", t=4)
+            for u in range(2):
+                ps = banks.tile([P, 2, TOK], F32, tag="bank", name="ps%d_%d" % (c, u))
+                for e in range(2):
+                    j = 2 * u + e
+                    col = D * x + 512 * grp + P * j
+                    for g in range(KG):
+                        nc.tensor.matmul_mx(
+                            out=ps[:, e, :],
+                            lhsT=w_sb[c][:, g, P * j : P * (j + 1)].bitcast(FP8X4),
+                            lhsT_scale=planes[4 * g : P, col : col + P],
+                            rhs=h_words[:, g, :].bitcast(FP8X4),
+                            rhs_scale=h_scale[:, g, :],
+                            start=(g == 0),
+                            stop=(g == KG - 1),
+                        )
+                dst = gview[:, :, 2 * u : 2 * u + 2]
+                src = ps[:].rearrange("p e w -> p w e")
+                if x == 0:
+                    nc.scalar.copy(out=dst, in_=src)
+                else:
+                    nc.vector.tensor_copy(out=dst, in_=src)
+            nc.vector.quantize_mx(out=x_words[c][:].bitcast(FP8X4), scales=x_scale[c][:], in_=grouped[:])
+
+        def scores(grp):
+            cq, ck = 2 * grp, 2 * grp + 1
+            for b in range(B):
+                cols = slice(P * b, P * (b + 1))
+                for first, (l, r) in enumerate(((cq, ck), (ck, cq))):
+                    nc.tensor.matmul_mx(
+                        out=lg[b][:],
+                        lhsT=x_words[l][:, cols].bitcast(FP8X4),
+                        lhsT_scale=x_scale[l][:, cols],
+                        rhs=x_words[r][:, cols].bitcast(FP8X4),
+                        rhs_scale=x_scale[r][:, cols],
+                        start=(grp == 0 and first == 0),
+                        stop=(grp == DG - 1 and first == 1),
+                    )
+
+        for grp in range(DG):
+            project(2 * grp)
+            if grp > 0:
+                scores(grp - 1)
+            project(2 * grp + 1)
+        scores(DG - 1)
+
+        y = keep.tile([P, B, P], F32, name="y")
+        ex = keep.tile([P, B, P], F32, name="ex")
+        res = keep.tile([P, B, P], F32, name="res")
+        nmax = keep.tile([P, B], F32, name="nmax")
+        ssum = keep.tile([P, B], F32, name="ssum")
+        rsum = keep.tile([P, B], F32, name="rsum")
+        cneg = -0.5 / (math.sqrt(C) * TAU)
+        for b in range(B):
+            nc.vector.scalar_tensor_tensor(
+                out=y[:, b, :], in0=lg[b][:], scalar=cneg, in1=neg_b[:], op0=ALU.mult, op1=ALU.add
+            )
+            nc.vector.tensor_reduce(out=nmax[:, b : b + 1], in_=y[:, b, :], axis=mybir.AxisListType.X, op=ALU.min)
+            nc.scalar.activation(
+                out=ex[:, b, :], in_=y[:, b, :], func=ACT.Exp, bias=nmax[:, b : b + 1], scale=-1.0,
+                accum_out=ssum[:, b : b + 1],
+            )
+        for b in range(B):
+            nc.vector.reciprocal(out=rsum[:, b : b + 1], in_=ssum[:, b : b + 1])
+            nc.vector.tensor_scalar(
+                out=res[:, b, :], in0=ex[:, b, :], scalar1=rsum[:, b : b + 1], scalar2=None, op0=ALU.mult
+            )
+            nc.sync.dma_start(out=out[b], in_=res[:, b, :])

@@ -24,6 +24,7 @@ KG = C // 512
 DG = D // 512
 TAU = 1.5
 BIG = 1.0e30
+PIECES = (2, 1, 1, 1, 1, 1, 1, 1)
 
 FLOPS = 2 * 2 * B * P * C * D + 2 * B * P * P * D
 
@@ -42,80 +43,103 @@ def tile_dynamicgraphattention_w_kernel(
         ctx.enter_context(tc.manual_schedule())
 
         planes = keep.tile([P, 2 * D], U8, align_bytes=64, name="planes")
-        h_sb = [keep.tile([P, C], BF16, name="h_sb%d" % b) for b in range(B)]
-        w_sb = [keep.tile([P, KG, 512], U32, align_bytes=64, name="w_sb%d" % c) for c in range(2 * DG)]
+        h_sb = [keep.tile([P, B, C // 2], BF16, name="h_sb%d" % s) for s in range(2)]
+        w_sb = [
+            [
+                keep.tile([P, KG, 512 // PIECES[c]], U32, align_bytes=64, name="w_sb%d_%d" % (c, i))
+                for i in range(PIECES[c])
+            ]
+            for c in range(2 * DG)
+        ]
+        zeros = keep.tile([P, 512], BF16, name="zeros")
         a_bf = keep.tile([P, P], BF16, name="a_bf")
         m_bf = keep.tile([P, P], BF16, name="m_bf")
         ident = keep.tile([P, P], F32, name="ident")
         warm = keep.tile([P, 1], F32, name="warm")
         warm2 = keep.tile([P, 1], F32, name="warm2")
 
+        nc.vector.memset(zeros[:].bitcast(I32), 0)
+        nc.vector.memset(ident[:], 0.0)
         nc.vector.memset(planes[:].bitcast(I32), 0)
         nc.vector.memset(warm[:], 0.0)
-        nc.scalar.activation(out=warm2[:], in_=warm[:], func=ACT.Exp)
-        make_identity(nc, ident[:])
-        nc.gpsimd.dma_start(out=a_bf[:], in_=A_stat)
-        nc.gpsimd.dma_start(out=m_bf[:], in_=M_mask)
+        make_identity(nc, ident[:], nomemset=True)
 
         def load_scales(x):
+            queue = nc.scalar if x == 0 else nc.gpsimd
             for q in range(4):
-                nc.sync.dma_start(
-                    out=planes[32 * q : 32 * q + 16, D * x : D * (x + 1)].bitcast(I32),
-                    in_=scales[x][:, 4 * q : 4 * q + 4, :].bitcast(I32),
+                queue.dma_start(
+                    out=planes[32 * q : 32 * q + 16, D * x : D * (x + 1)].bitcast(F32),
+                    in_=scales[x][:, 4 * q : 4 * q + 4, :].bitcast(F32),
                 )
 
         def load_words(c):
             x, grp = c % 2, c // 2
             src = words[x].rearrange("g p n t -> p g (n t)")
-            nc.sync.dma_start(
-                out=w_sb[c][:].bitcast(I32),
-                in_=src[:, :, 2048 * grp : 2048 * (grp + 1)].bitcast(I32),
-            )
+            width = 2048 // PIECES[c]
+            for i in range(PIECES[c]):
+                lo = 2048 * grp + width * i
+                nc.sync.dma_start(out=w_sb[c][i][:].bitcast(I32), in_=src[:, :, lo : lo + width].bitcast(I32))
 
-        for b in range(B):
-            nc.sync.dma_start(out=h_sb[b][:], in_=H_t[b])
+        h_src = H_t.rearrange("b n c -> n b c")
+        for s in range(2):
+            nc.sync.dma_start(out=h_sb[s][:], in_=h_src[:, :, (C // 2) * s : (C // 2) * (s + 1)])
         load_scales(0)
-        load_words(0)
         load_scales(1)
-        for c in range(1, 2 * DG):
+        nc.gpsimd.dma_start(out=a_bf[:], in_=A_stat)
+        nc.gpsimd.dma_start(out=m_bf[:], in_=M_mask)
+        for c in range(2 * DG):
             load_words(c)
+        nc.scalar.activation(out=warm2[:], in_=warm[:], func=ACT.Exp)
+
+        idle = banks.tile([P, 512], F32, tag="bank", name="idle")
+
+        def spin(n):
+            for i in range(n):
+                nc.tensor.matmul(out=idle[:], lhsT=zeros[:, 0:P], rhs=zeros[:], start=True, stop=True)
+
+        spin(6)
 
         h_words = keep.tile([P, KG, TOK], U32, align_bytes=64, name="h_words")
         h_scale = keep.tile([P, KG, TOK], U8, align_bytes=64, name="h_scale")
         h_grp = [keep.tile([P, 4 * TOK], BF16, align_bytes=64, name="h_grp%d" % g) for g in range(KG)]
         xt = [banks.tile([P, 2, TOK], F32, tag="bank", name="xt%d" % g) for g in range(KG)]
-        for b in range(B):
-            hw32 = h_sb[b][:].bitcast(F32)
-            for g in range(KG):
+        def h_transposes(g):
+            for b in range(B):
+                hw32 = h_sb[g // 2][:, b, :].bitcast(F32)
                 for u in range(2):
                     nc.tensor.transpose(
                         xt[g][:, u, P * b : P * (b + 1)],
-                        hw32[:, 256 * g + u : 256 * (g + 1) : 2],
+                        hw32[:, 256 * (g % 2) + u : 256 * (g % 2 + 1) : 2],
                         ident[:],
                     )
-        for g in (0, 2, 1, 3):
+
+        def h_copy(g):
             dst = h_grp[g][:].bitcast(F32).rearrange("p (w u) -> p w u", u=2)
             src = xt[g][:].rearrange("p u w -> p w u")
             if g % 2 == 0:
                 nc.vector.tensor_copy(out=dst, in_=src)
             else:
                 nc.scalar.copy(out=dst, in_=src)
-        for g in range(KG):
+
+        def h_quantise(g):
             nc.vector.quantize_mx(
                 out=h_words[:, g, :].bitcast(FP8X4), scales=h_scale[:, g, :], in_=h_grp[g][:]
             )
 
-        not_i = keep.tile([P, P], F32, name="not_i")
-        allowed = keep.tile([P, P], F32, name="allowed")
-        a_keep = keep.tile([P, P], F32, name="a_keep")
-        neg_b = keep.tile([P, P], F32, name="neg_b")
-        nc.vector.tensor_scalar(out=not_i[:], in0=ident[:], scalar1=-1.0, scalar2=1.0, op0=ALU.mult, op1=ALU.add)
-        nc.vector.scalar_tensor_tensor(
-            out=allowed[:], in0=m_bf[:], scalar=0.0, in1=not_i[:], op0=ALU.is_gt, op1=ALU.mult
-        )
-        nc.vector.tensor_tensor(out=a_keep[:], in0=a_bf[:], in1=allowed[:], op=ALU.mult)
-        nc.vector.tensor_scalar(out=neg_b[:], in0=allowed[:], scalar1=-BIG, scalar2=BIG, op0=ALU.mult, op1=ALU.add)
-        nc.vector.tensor_tensor(out=neg_b[:], in0=neg_b[:], in1=a_keep[:], op=ALU.subtract)
+        h_transposes(0)
+        h_transposes(1)
+        spin(1)
+        h_transposes(2)
+        h_transposes(3)
+        spin(4)
+        h_copy(0)
+        h_copy(1)
+        h_quantise(0)
+        h_copy(2)
+        h_copy(3)
+        h_quantise(1)
+        h_quantise(2)
+        h_quantise(3)
 
         x_words = [keep.tile([P, TOK], U32, align_bytes=64, name="x_words%d" % c) for c in range(2 * DG)]
         x_scale = [keep.tile([P, TOK], U8, align_bytes=64, name="x_scale%d" % c) for c in range(2 * DG)]
@@ -130,10 +154,11 @@ def tile_dynamicgraphattention_w_kernel(
                 for e in range(2):
                     j = 2 * u + e
                     col = D * x + 512 * grp + P * j
+                    wcol = P * (j % (4 // PIECES[c]))
                     for g in range(KG):
                         nc.tensor.matmul_mx(
                             out=ps[:, e, :],
-                            lhsT=w_sb[c][:, g, P * j : P * (j + 1)].bitcast(FP8X4),
+                            lhsT=w_sb[c][j * PIECES[c] // 4][:, g, wcol : wcol + P].bitcast(FP8X4),
                             lhsT_scale=planes[4 * g : P, col : col + P],
                             rhs=h_words[:, g, :].bitcast(FP8X4),
                             rhs_scale=h_scale[:, g, :],
@@ -163,12 +188,26 @@ def tile_dynamicgraphattention_w_kernel(
                         stop=(grp == DG - 1 and first == 1),
                     )
 
+        not_i = keep.tile([P, P], F32, name="not_i")
+        allowed = keep.tile([P, P], F32, name="allowed")
+        a_keep = keep.tile([P, P], F32, name="a_keep")
+        neg_b = keep.tile([P, P], F32, name="neg_b")
+
+        def build_mask():
+            nc.vector.tensor_scalar(out=not_i[:], in0=ident[:], scalar1=-1.0, scalar2=1.0, op0=ALU.mult, op1=ALU.add)
+            nc.vector.scalar_tensor_tensor(
+                out=allowed[:], in0=m_bf[:], scalar=0.0, in1=not_i[:], op0=ALU.is_gt, op1=ALU.mult
+            )
+            nc.vector.tensor_tensor(out=a_keep[:], in0=a_bf[:], in1=allowed[:], op=ALU.mult)
+            nc.vector.tensor_scalar(out=neg_b[:], in0=allowed[:], scalar1=-BIG, scalar2=BIG, op0=ALU.mult, op1=ALU.add)
+            nc.vector.tensor_tensor(out=neg_b[:], in0=neg_b[:], in1=a_keep[:], op=ALU.subtract)
+
+        for c in range(2 * DG):
+            project(c)
+            if c == 1:
+                build_mask()
         for grp in range(DG):
-            project(2 * grp)
-            if grp > 0:
-                scores(grp - 1)
-            project(2 * grp + 1)
-        scores(DG - 1)
+            scores(grp)
 
         y = keep.tile([P, B, P], F32, name="y")
         ex = keep.tile([P, B, P], F32, name="ex")

@@ -1,9 +1,7 @@
 from contextlib import ExitStack
 import math
 
-import concourse.bass as bass
 import concourse.mybir as mybir
-import concourse.tile as tile
 from concourse.masks import make_identity
 
 F32 = mybir.dt.float32
@@ -22,9 +20,12 @@ D = 2048
 TOK = B * P
 KG = C // 512
 DG = D // 512
+NCH = 2 * DG
 TAU = 1.5
 BIG = 1.0e30
-PIECES = (2, 1, 1, 1, 1, 1, 1, 1)
+FINE = ((0,), (1,), (2,), (3,))
+PAIRS = ((0, 1), (2, 3))
+SLICES = (FINE, PAIRS, PAIRS, PAIRS, PAIRS, PAIRS, FINE, FINE)
 
 FLOPS = 2 * 2 * B * P * C * D + 2 * B * P * P * D
 
@@ -37,19 +38,18 @@ def tile_dynamicgraphattention_w_kernel(
     scales = (Wq_scales, Wk_scales)
     with ExitStack() as ctx:
         keep = ctx.enter_context(tc.tile_pool(name="keep", bufs=1))
-        ring = ctx.enter_context(tc.tile_pool(name="ring", bufs=4))
-        banks = ctx.enter_context(tc.psum_pool(name="banks", bufs=6))
-        lgp = ctx.enter_context(tc.psum_pool(name="lgp", bufs=1))
+        ring = ctx.enter_context(tc.tile_pool(name="ring", bufs=3))
+        banks = ctx.enter_context(tc.psum_pool(name="banks", bufs=8))
         ctx.enter_context(tc.manual_schedule())
 
         planes = keep.tile([P, 2 * D], U8, align_bytes=64, name="planes")
         h_sb = [keep.tile([P, B, C // 2], BF16, name="h_sb%d" % s) for s in range(2)]
         w_sb = [
             [
-                keep.tile([P, KG, 512 // PIECES[c]], U32, align_bytes=64, name="w_sb%d_%d" % (c, i))
-                for i in range(PIECES[c])
+                keep.tile([P, len(gs), 512], U32, align_bytes=64, name="w_sb%d_%d" % (c, i))
+                for i, gs in enumerate(SLICES[c])
             ]
-            for c in range(2 * DG)
+            for c in range(NCH)
         ]
         zeros = keep.tile([P, 512], BF16, name="zeros")
         a_bf = keep.tile([P, P], BF16, name="a_bf")
@@ -65,31 +65,30 @@ def tile_dynamicgraphattention_w_kernel(
         make_identity(nc, ident[:], nomemset=True)
 
         def load_scales(x):
-            queue = nc.scalar if x == 0 else nc.gpsimd
             for q in range(4):
-                queue.dma_start(
+                nc.scalar.dma_start(
                     out=planes[32 * q : 32 * q + 16, D * x : D * (x + 1)].bitcast(F32),
                     in_=scales[x][:, 4 * q : 4 * q + 4, :].bitcast(F32),
                 )
 
-        def load_words(c):
-            x, grp = c % 2, c // 2
+        def load_words(c, i):
+            x, grp = c // DG, c % DG
+            gs = SLICES[c][i]
             src = words[x].rearrange("g p n t -> p g (n t)")
-            width = 2048 // PIECES[c]
-            for i in range(PIECES[c]):
-                lo = 2048 * grp + width * i
-                nc.sync.dma_start(out=w_sb[c][i][:].bitcast(I32), in_=src[:, :, lo : lo + width].bitcast(I32))
+            nc.sync.dma_start(
+                out=w_sb[c][i][:].bitcast(I32),
+                in_=src[:, gs[0] : gs[-1] + 1, 2048 * grp : 2048 * (grp + 1)].bitcast(I32),
+            )
 
         h_src = H_t.rearrange("b n c -> n b c")
         for s in range(2):
             nc.sync.dma_start(out=h_sb[s][:], in_=h_src[:, :, (C // 2) * s : (C // 2) * (s + 1)])
         load_scales(0)
-        load_scales(1)
+        nc.scalar.activation(out=warm2[:], in_=warm[:], func=ACT.Exp)
         nc.gpsimd.dma_start(out=a_bf[:], in_=A_stat)
         nc.gpsimd.dma_start(out=m_bf[:], in_=M_mask)
-        for c in range(2 * DG):
-            load_words(c)
-        nc.scalar.activation(out=warm2[:], in_=warm[:], func=ACT.Exp)
+        load_words(0, 0)
+        load_words(0, 1)
 
         idle = banks.tile([P, 512], F32, tag="bank", name="idle")
 
@@ -103,6 +102,7 @@ def tile_dynamicgraphattention_w_kernel(
         h_scale = keep.tile([P, KG, TOK], U8, align_bytes=64, name="h_scale")
         h_grp = [keep.tile([P, 4 * TOK], BF16, align_bytes=64, name="h_grp%d" % g) for g in range(KG)]
         xt = [banks.tile([P, 2, TOK], F32, tag="bank", name="xt%d" % g) for g in range(KG)]
+
         def h_transposes(g):
             for b in range(B):
                 hw32 = h_sb[g // 2][:, b, :].bitcast(F32)
@@ -131,7 +131,6 @@ def tile_dynamicgraphattention_w_kernel(
         spin(1)
         h_transposes(2)
         h_transposes(3)
-        spin(4)
         h_copy(0)
         h_copy(1)
         h_quantise(0)
@@ -141,52 +140,44 @@ def tile_dynamicgraphattention_w_kernel(
         h_quantise(2)
         h_quantise(3)
 
-        x_words = [keep.tile([P, TOK], U32, align_bytes=64, name="x_words%d" % c) for c in range(2 * DG)]
-        x_scale = [keep.tile([P, TOK], U8, align_bytes=64, name="x_scale%d" % c) for c in range(2 * DG)]
-        lg = [lgp.tile([P, P], F32, name="lg%d" % b) for b in range(B)]
+        load_words(0, 2)
+        load_words(0, 3)
+        load_scales(1)
+        for c in range(1, NCH):
+            for i in range(len(SLICES[c])):
+                load_words(c, i)
+
+        x_words = [keep.tile([P, TOK], U32, align_bytes=64, name="x_words%d" % c) for c in range(NCH)]
+        x_scale = [keep.tile([P, TOK], U8, align_bytes=64, name="x_scale%d" % c) for c in range(NCH)]
 
         def project(c):
-            x, grp = c % 2, c // 2
-            grouped = ring.tile([P, 4 * TOK], BF16, align_bytes=64, tag="grouped", name="grouped%d" % c)
-            gview = grouped[:].rearrange("p (w t) -> p w t", t=4)
-            for u in range(2):
-                ps = banks.tile([P, 2, TOK], F32, tag="bank", name="ps%d_%d" % (c, u))
-                for e in range(2):
-                    j = 2 * u + e
-                    col = D * x + 512 * grp + P * j
-                    wcol = P * (j % (4 // PIECES[c]))
-                    for g in range(KG):
+            x, grp = c // DG, c % DG
+            ps = [banks.tile([P, TOK], F32, tag="bank", name="ps%d_%d" % (c, t)) for t in range(4)]
+            for i, gs in enumerate(SLICES[c]):
+                for t in range(4):
+                    col = D * x + 512 * grp + P * t
+                    for k, g in enumerate(gs):
                         nc.tensor.matmul_mx(
-                            out=ps[:, e, :],
-                            lhsT=w_sb[c][j * PIECES[c] // 4][:, g, wcol : wcol + P].bitcast(FP8X4),
+                            out=ps[t][:],
+                            lhsT=w_sb[c][i][:, k, P * t : P * (t + 1)].bitcast(FP8X4),
                             lhsT_scale=planes[4 * g : P, col : col + P],
                             rhs=h_words[:, g, :].bitcast(FP8X4),
                             rhs_scale=h_scale[:, g, :],
                             start=(g == 0),
                             stop=(g == KG - 1),
                         )
-                dst = gview[:, :, 2 * u : 2 * u + 2]
-                src = ps[:].rearrange("p e w -> p w e")
-                if x == 0:
-                    nc.scalar.copy(out=dst, in_=src)
+            stage = ring.tile([P, 4, TOK], BF16, tag="stage", name="stage%d" % c)
+            grouped = ring.tile([P, 4 * TOK], BF16, align_bytes=64, tag="grouped", name="grouped%d" % c)
+            for t in range(4):
+                if t < 2:
+                    nc.scalar.copy(out=stage[:, t, :], in_=ps[t][:])
                 else:
-                    nc.vector.tensor_copy(out=dst, in_=src)
+                    nc.vector.tensor_copy(out=stage[:, t, :], in_=ps[t][:])
+            nc.vector.tensor_copy(
+                out=grouped[:].rearrange("p (c i t) -> p c t i", i=4, t=4),
+                in_=stage[:].rearrange("p t (c i) -> p c t i", i=4),
+            )
             nc.vector.quantize_mx(out=x_words[c][:].bitcast(FP8X4), scales=x_scale[c][:], in_=grouped[:])
-
-        def scores(grp):
-            cq, ck = 2 * grp, 2 * grp + 1
-            for b in range(B):
-                cols = slice(P * b, P * (b + 1))
-                for first, (l, r) in enumerate(((cq, ck), (ck, cq))):
-                    nc.tensor.matmul_mx(
-                        out=lg[b][:],
-                        lhsT=x_words[l][:, cols].bitcast(FP8X4),
-                        lhsT_scale=x_scale[l][:, cols],
-                        rhs=x_words[r][:, cols].bitcast(FP8X4),
-                        rhs_scale=x_scale[r][:, cols],
-                        start=(grp == 0 and first == 0),
-                        stop=(grp == DG - 1 and first == 1),
-                    )
 
         not_i = keep.tile([P, P], F32, name="not_i")
         allowed = keep.tile([P, P], F32, name="allowed")
@@ -202,12 +193,26 @@ def tile_dynamicgraphattention_w_kernel(
             nc.vector.tensor_scalar(out=neg_b[:], in0=allowed[:], scalar1=-BIG, scalar2=BIG, op0=ALU.mult, op1=ALU.add)
             nc.vector.tensor_tensor(out=neg_b[:], in0=neg_b[:], in1=a_keep[:], op=ALU.subtract)
 
-        for c in range(2 * DG):
+        for c in range(NCH):
             project(c)
-            if c == 1:
+            if c == 3:
                 build_mask()
+
+        lg = [banks.tile([P, P], F32, tag="bank", name="lg%d" % b) for b in range(B)]
         for grp in range(DG):
-            scores(grp)
+            cq, ck = grp, DG + grp
+            for b in range(B):
+                cols = slice(P * b, P * (b + 1))
+                for second, (l, r) in enumerate(((cq, ck), (ck, cq))):
+                    nc.tensor.matmul_mx(
+                        out=lg[b][:],
+                        lhsT=x_words[l][:, cols].bitcast(FP8X4),
+                        lhsT_scale=x_scale[l][:, cols],
+                        rhs=x_words[r][:, cols].bitcast(FP8X4),
+                        rhs_scale=x_scale[r][:, cols],
+                        start=(grp == 0 and second == 0),
+                        stop=(grp == DG - 1 and second == 1),
+                    )
 
         y = keep.tile([P, B, P], F32, name="y")
         ex = keep.tile([P, B, P], F32, name="ex")

@@ -23,9 +23,7 @@ DG = D // 512
 NCH = 2 * DG
 TAU = 1.5
 BIG = 1.0e30
-FINE = ((0,), (1,), (2,), (3,))
-PAIRS = ((0, 1), (2, 3))
-SLICES = (FINE, PAIRS, PAIRS, PAIRS, PAIRS, PAIRS, FINE, FINE)
+PIECES = (2, 1, 1, 1, 1, 1, 1, 1)
 
 FLOPS = 2 * 2 * B * P * C * D + 2 * B * P * P * D
 
@@ -39,15 +37,15 @@ def tile_dynamicgraphattention_w_kernel(
     with ExitStack() as ctx:
         keep = ctx.enter_context(tc.tile_pool(name="keep", bufs=1))
         ring = ctx.enter_context(tc.tile_pool(name="ring", bufs=3))
-        banks = ctx.enter_context(tc.psum_pool(name="banks", bufs=8))
+        banks = ctx.enter_context(tc.psum_pool(name="banks", bufs=1))
         ctx.enter_context(tc.manual_schedule())
 
         planes = keep.tile([P, 2 * D], U8, align_bytes=64, name="planes")
         h_sb = [keep.tile([P, B, C // 2], BF16, name="h_sb%d" % s) for s in range(2)]
         w_sb = [
             [
-                keep.tile([P, len(gs), 512], U32, align_bytes=64, name="w_sb%d_%d" % (c, i))
-                for i, gs in enumerate(SLICES[c])
+                keep.tile([P, KG, 512 // PIECES[c]], U32, align_bytes=64, name="w_sb%d_%d" % (c, i))
+                for i in range(PIECES[c])
             ]
             for c in range(NCH)
         ]
@@ -73,12 +71,10 @@ def tile_dynamicgraphattention_w_kernel(
 
         def load_words(c, i):
             x, grp = c // DG, c % DG
-            gs = SLICES[c][i]
             src = words[x].rearrange("g p n t -> p g (n t)")
-            nc.sync.dma_start(
-                out=w_sb[c][i][:].bitcast(I32),
-                in_=src[:, gs[0] : gs[-1] + 1, 2048 * grp : 2048 * (grp + 1)].bitcast(I32),
-            )
+            width = 2048 // PIECES[c]
+            lo = 2048 * grp + width * i
+            nc.sync.dma_start(out=w_sb[c][i][:].bitcast(I32), in_=src[:, :, lo : lo + width].bitcast(I32))
 
         h_src = H_t.rearrange("b n c -> n b c")
         for s in range(2):
@@ -90,7 +86,7 @@ def tile_dynamicgraphattention_w_kernel(
         load_words(0, 0)
         load_words(0, 1)
 
-        idle = banks.tile([P, 512], F32, tag="bank", name="idle")
+        idle = banks.tile([P, 512], F32, tag="bank7", name="idle")
 
         def spin(n):
             for i in range(n):
@@ -101,7 +97,7 @@ def tile_dynamicgraphattention_w_kernel(
         h_words = keep.tile([P, KG, TOK], U32, align_bytes=64, name="h_words")
         h_scale = keep.tile([P, KG, TOK], U8, align_bytes=64, name="h_scale")
         h_grp = [keep.tile([P, 4 * TOK], BF16, align_bytes=64, name="h_grp%d" % g) for g in range(KG)]
-        xt = [banks.tile([P, 2, TOK], F32, tag="bank", name="xt%d" % g) for g in range(KG)]
+        xt = [banks.tile([P, 2, TOK], F32, tag="bank%d" % g, name="xt%d" % g) for g in range(KG)]
 
         def h_transposes(g):
             for b in range(B):
@@ -140,43 +136,40 @@ def tile_dynamicgraphattention_w_kernel(
         h_quantise(2)
         h_quantise(3)
 
-        load_words(0, 2)
-        load_words(0, 3)
+        load_words(1, 0)
         load_scales(1)
-        for c in range(1, NCH):
-            for i in range(len(SLICES[c])):
-                load_words(c, i)
+        for c in range(2, NCH):
+            load_words(c, 0)
 
         x_words = [keep.tile([P, TOK], U32, align_bytes=64, name="x_words%d" % c) for c in range(NCH)]
         x_scale = [keep.tile([P, TOK], U8, align_bytes=64, name="x_scale%d" % c) for c in range(NCH)]
 
         def project(c):
             x, grp = c // DG, c % DG
-            ps = [banks.tile([P, TOK], F32, tag="bank", name="ps%d_%d" % (c, t)) for t in range(4)]
-            for i, gs in enumerate(SLICES[c]):
-                for t in range(4):
-                    col = D * x + 512 * grp + P * t
-                    for k, g in enumerate(gs):
+            grouped = ring.tile([P, 4 * TOK], BF16, align_bytes=64, tag="grouped", name="grouped%d" % c)
+            gview = grouped[:].rearrange("p (w t) -> p w t", t=4)
+            for u in range(2):
+                ps = banks.tile([P, 2, TOK], F32, tag="bank%d" % ((4 + 2 * c + u) % 8), name="ps%d_%d" % (c, u))
+                for e in range(2):
+                    j = 2 * u + e
+                    col = D * x + 512 * grp + P * j
+                    wcol = P * (j % (4 // PIECES[c]))
+                    for g in range(KG):
                         nc.tensor.matmul_mx(
-                            out=ps[t][:],
-                            lhsT=w_sb[c][i][:, k, P * t : P * (t + 1)].bitcast(FP8X4),
+                            out=ps[:, e, :],
+                            lhsT=w_sb[c][j * PIECES[c] // 4][:, g, wcol : wcol + P].bitcast(FP8X4),
                             lhsT_scale=planes[4 * g : P, col : col + P],
                             rhs=h_words[:, g, :].bitcast(FP8X4),
                             rhs_scale=h_scale[:, g, :],
                             start=(g == 0),
                             stop=(g == KG - 1),
                         )
-            stage = ring.tile([P, 4, TOK], BF16, tag="stage", name="stage%d" % c)
-            grouped = ring.tile([P, 4 * TOK], BF16, align_bytes=64, tag="grouped", name="grouped%d" % c)
-            for t in range(4):
-                if t < 2:
-                    nc.scalar.copy(out=stage[:, t, :], in_=ps[t][:])
+                dst = gview[:, :, 2 * u : 2 * u + 2]
+                src = ps[:].rearrange("p e w -> p w e")
+                if c % 2 == 0:
+                    nc.scalar.copy(out=dst, in_=src)
                 else:
-                    nc.vector.tensor_copy(out=stage[:, t, :], in_=ps[t][:])
-            nc.vector.tensor_copy(
-                out=grouped[:].rearrange("p (c i t) -> p c t i", i=4, t=4),
-                in_=stage[:].rearrange("p t (c i) -> p c t i", i=4),
-            )
+                    nc.vector.tensor_copy(out=dst, in_=src)
             nc.vector.quantize_mx(out=x_words[c][:].bitcast(FP8X4), scales=x_scale[c][:], in_=grouped[:])
 
         not_i = keep.tile([P, P], F32, name="not_i")
@@ -198,7 +191,7 @@ def tile_dynamicgraphattention_w_kernel(
             if c == 3:
                 build_mask()
 
-        lg = [banks.tile([P, P], F32, tag="bank", name="lg%d" % b) for b in range(B)]
+        lg = [banks.tile([P, P], F32, tag="bank%d" % (4 + b), name="lg%d" % b) for b in range(B)]
         for grp in range(DG):
             cq, ck = grp, DG + grp
             for b in range(B):

@@ -23,7 +23,7 @@ DG = D // 512
 NCH = 2 * DG
 TAU = 1.5
 BIG = 1.0e30
-PIECES = (2, 1, 1, 1, 1, 1, 1, 1)
+PLAN = ((4, 4, 4, 4), (4, 4, 3, 2, 2, 1))
 
 FLOPS = 2 * 2 * B * P * C * D + 2 * B * P * P * D
 
@@ -43,12 +43,10 @@ def tile_dynamicgraphattention_w_kernel(
         planes = keep.tile([P, 2 * D], U8, align_bytes=64, name="planes")
         h_sb = [keep.tile([P, B, C // 2], BF16, name="h_sb%d" % s) for s in range(2)]
         w_sb = [
-            [
-                keep.tile([P, KG, 512 // PIECES[c]], U32, align_bytes=64, name="w_sb%d_%d" % (c, i))
-                for i in range(PIECES[c])
-            ]
-            for c in range(NCH)
+            [keep.tile([P, KG, P * n], U32, align_bytes=64, name="w_sb%d_%d" % (x, i)) for i, n in enumerate(PLAN[x])]
+            for x in range(2)
         ]
+        where = [[(i, j) for i, n in enumerate(PLAN[x]) for j in range(n)] for x in range(2)]
         zeros = keep.tile([P, 512], BF16, name="zeros")
         a_bf = keep.tile([P, P], BF16, name="a_bf")
         m_bf = keep.tile([P, P], BF16, name="m_bf")
@@ -56,35 +54,37 @@ def tile_dynamicgraphattention_w_kernel(
         warm = keep.tile([P, 1], F32, name="warm")
         warm2 = keep.tile([P, 1], F32, name="warm2")
 
-        nc.vector.memset(zeros[:].bitcast(I32), 0)
         nc.vector.memset(ident[:], 0.0)
         nc.vector.memset(planes[:].bitcast(I32), 0)
+        nc.vector.memset(zeros[:].bitcast(I32), 0)
         nc.vector.memset(warm[:], 0.0)
         make_identity(nc, ident[:], nomemset=True)
 
-        def load_scales(x):
+        def load_scales(queue, x, lo, hi):
             for q in range(4):
-                nc.scalar.dma_start(
-                    out=planes[32 * q : 32 * q + 16, D * x : D * (x + 1)].bitcast(F32),
-                    in_=scales[x][:, 4 * q : 4 * q + 4, :].bitcast(F32),
+                queue.dma_start(
+                    out=planes[32 * q : 32 * q + 16, D * x + lo : D * x + hi].bitcast(F32),
+                    in_=scales[x][:, 4 * q : 4 * q + 4, lo:hi].bitcast(F32),
                 )
 
-        def load_words(c, i):
-            x, grp = c // DG, c % DG
+        def load_words(x):
             src = words[x].rearrange("g p n t -> p g (n t)")
-            width = 2048 // PIECES[c]
-            lo = 2048 * grp + width * i
-            nc.sync.dma_start(out=w_sb[c][i][:].bitcast(I32), in_=src[:, :, lo : lo + width].bitcast(I32))
+            lo = 0
+            for i, n in enumerate(PLAN[x]):
+                nc.sync.dma_start(out=w_sb[x][i][:].bitcast(I32), in_=src[:, :, lo : lo + 512 * n].bitcast(I32))
+                lo += 512 * n
 
         h_src = H_t.rearrange("b n c -> n b c")
         for s in range(2):
             nc.sync.dma_start(out=h_sb[s][:], in_=h_src[:, :, (C // 2) * s : (C // 2) * (s + 1)])
-        load_scales(0)
+        load_scales(nc.scalar, 0, 0, 512)
         nc.scalar.activation(out=warm2[:], in_=warm[:], func=ACT.Exp)
+        load_scales(nc.gpsimd, 0, 512, D)
+        load_scales(nc.gpsimd, 1, 0, D)
         nc.gpsimd.dma_start(out=a_bf[:], in_=A_stat)
         nc.gpsimd.dma_start(out=m_bf[:], in_=M_mask)
-        load_words(0, 0)
-        load_words(0, 1)
+        load_words(0)
+        load_words(1)
 
         idle = banks.tile([P, 512], F32, tag="bank7", name="idle")
 
@@ -136,13 +136,22 @@ def tile_dynamicgraphattention_w_kernel(
         h_quantise(2)
         h_quantise(3)
 
-        load_words(1, 0)
-        load_scales(1)
-        for c in range(2, NCH):
-            load_words(c, 0)
-
         x_words = [keep.tile([P, TOK], U32, align_bytes=64, name="x_words%d" % c) for c in range(NCH)]
         x_scale = [keep.tile([P, TOK], U8, align_bytes=64, name="x_scale%d" % c) for c in range(NCH)]
+
+        def passes(x, blk, dst, tok):
+            i, j = where[x][blk]
+            col = D * x + P * blk
+            for g in range(KG):
+                nc.tensor.matmul_mx(
+                    out=dst,
+                    lhsT=w_sb[x][i][:, g, P * j : P * (j + 1)].bitcast(FP8X4),
+                    lhsT_scale=planes[4 * g : P, col : col + P],
+                    rhs=h_words[:, g, tok].bitcast(FP8X4),
+                    rhs_scale=h_scale[:, g, tok],
+                    start=(g == 0),
+                    stop=(g == KG - 1),
+                )
 
         def project(c):
             x, grp = c // DG, c % DG
@@ -151,19 +160,7 @@ def tile_dynamicgraphattention_w_kernel(
             for u in range(2):
                 ps = banks.tile([P, 2, TOK], F32, tag="bank%d" % ((4 + 2 * c + u) % 8), name="ps%d_%d" % (c, u))
                 for e in range(2):
-                    j = 2 * u + e
-                    col = D * x + 512 * grp + P * j
-                    wcol = P * (j % (4 // PIECES[c]))
-                    for g in range(KG):
-                        nc.tensor.matmul_mx(
-                            out=ps[:, e, :],
-                            lhsT=w_sb[c][j * PIECES[c] // 4][:, g, wcol : wcol + P].bitcast(FP8X4),
-                            lhsT_scale=planes[4 * g : P, col : col + P],
-                            rhs=h_words[:, g, :].bitcast(FP8X4),
-                            rhs_scale=h_scale[:, g, :],
-                            start=(g == 0),
-                            stop=(g == KG - 1),
-                        )
+                    passes(x, 4 * grp + 2 * u + e, ps[:, e, :], slice(0, TOK))
                 dst = gview[:, :, 2 * u : 2 * u + 2]
                 src = ps[:].rearrange("p e w -> p w e")
                 if c % 2 == 0:
@@ -171,6 +168,26 @@ def tile_dynamicgraphattention_w_kernel(
                 else:
                     nc.vector.tensor_copy(out=dst, in_=src)
             nc.vector.quantize_mx(out=x_words[c][:].bitcast(FP8X4), scales=x_scale[c][:], in_=grouped[:])
+
+        def project_last(c):
+            x, grp = c // DG, c % DG
+            ps = [banks.tile([P, 4, P], F32, tag="bank%d" % ((4 + 2 * c + b) % 8), name="pl%d" % b) for b in range(B)]
+            grouped = [keep.tile([P, 4 * P], BF16, align_bytes=64, name="glast%d" % b) for b in range(B)]
+            for t in range(4):
+                for b in range(B):
+                    passes(x, 4 * grp + t, ps[b][:, t, :], slice(P * b, P * (b + 1)))
+            for b in range(B):
+                dst = grouped[b][:].rearrange("p (w t) -> p w t", t=4)
+                src = ps[b][:].rearrange("p t w -> p w t")
+                if b == 0:
+                    nc.scalar.copy(out=dst, in_=src)
+                else:
+                    nc.vector.tensor_copy(out=dst, in_=src)
+            for b in range(B):
+                cols = slice(P * b, P * (b + 1))
+                nc.vector.quantize_mx(
+                    out=x_words[c][:, cols].bitcast(FP8X4), scales=x_scale[c][:, cols], in_=grouped[b][:]
+                )
 
         not_i = keep.tile([P, P], F32, name="not_i")
         allowed = keep.tile([P, P], F32, name="allowed")
@@ -186,10 +203,11 @@ def tile_dynamicgraphattention_w_kernel(
             nc.vector.tensor_scalar(out=neg_b[:], in0=allowed[:], scalar1=-BIG, scalar2=BIG, op0=ALU.mult, op1=ALU.add)
             nc.vector.tensor_tensor(out=neg_b[:], in0=neg_b[:], in1=a_keep[:], op=ALU.subtract)
 
-        for c in range(NCH):
+        for c in range(NCH - 1):
             project(c)
             if c == 3:
                 build_mask()
+        project_last(NCH - 1)
 
         lg = [banks.tile([P, P], F32, tag="bank%d" % (4 + b), name="lg%d" % b) for b in range(B)]
         for grp in range(DG):

@@ -23,7 +23,10 @@ DG = D // 512
 NCH = 2 * DG
 TAU = 1.5
 BIG = 1.0e30
-PLAN = ((4, 4, 4, 4), (4, 4, 3, 2, 2, 1))
+SETS = ((0, 0, 8, 4), (0, 8, 8, 0), (1, 0, 8, 4), (1, 8, 4, 0))
+LAST = (1, 12, 4, 2)
+LAST_CUT = (2, 1, 1)
+HEAD_COLS = 1024
 
 FLOPS = 2 * 2 * B * P * C * D + 2 * B * P * P * D
 
@@ -36,17 +39,13 @@ def tile_dynamicgraphattention_w_kernel(
     scales = (Wq_scales, Wk_scales)
     with ExitStack() as ctx:
         keep = ctx.enter_context(tc.tile_pool(name="keep", bufs=1))
-        ring = ctx.enter_context(tc.tile_pool(name="ring", bufs=3))
+        ring = ctx.enter_context(tc.tile_pool(name="ring", bufs=4))
         banks = ctx.enter_context(tc.psum_pool(name="banks", bufs=1))
         ctx.enter_context(tc.manual_schedule())
 
         planes = keep.tile([P, 2 * D], U8, align_bytes=64, name="planes")
         h_sb = [keep.tile([P, B, C // 2], BF16, name="h_sb%d" % s) for s in range(2)]
-        w_sb = [
-            [keep.tile([P, KG, P * n], U32, align_bytes=64, name="w_sb%d_%d" % (x, i)) for i, n in enumerate(PLAN[x])]
-            for x in range(2)
-        ]
-        where = [[(i, j) for i, n in enumerate(PLAN[x]) for j in range(n)] for x in range(2)]
+        w_sb = {}
         zeros = keep.tile([P, 512], BF16, name="zeros")
         a_bf = keep.tile([P, P], BF16, name="a_bf")
         m_bf = keep.tile([P, P], BF16, name="m_bf")
@@ -67,24 +66,31 @@ def tile_dynamicgraphattention_w_kernel(
                     in_=scales[x][:, 4 * q : 4 * q + 4, lo:hi].bitcast(F32),
                 )
 
-        def load_words(x):
+        def load_words(x, g, blk, n):
             src = words[x].rearrange("g p n t -> p g (n t)")
-            lo = 0
-            for i, n in enumerate(PLAN[x]):
-                nc.sync.dma_start(out=w_sb[x][i][:].bitcast(I32), in_=src[:, :, lo : lo + 512 * n].bitcast(I32))
-                lo += 512 * n
+            piece = keep.tile([P, P * n], U32, align_bytes=64, name="w_sb%d_%d_%d" % (x, g, blk))
+            nc.sync.dma_start(out=piece[:].bitcast(I32), in_=src[:, g, 512 * blk : 512 * (blk + n)].bitcast(I32))
+            for j in range(n):
+                w_sb[(x, g, blk + j)] = piece[:, P * j : P * (j + 1)]
 
         h_src = H_t.rearrange("b n c -> n b c")
         for s in range(2):
             nc.sync.dma_start(out=h_sb[s][:], in_=h_src[:, :, (C // 2) * s : (C // 2) * (s + 1)])
-        load_scales(nc.scalar, 0, 0, 512)
+        load_scales(nc.scalar, 0, 0, HEAD_COLS)
         nc.scalar.activation(out=warm2[:], in_=warm[:], func=ACT.Exp)
-        load_scales(nc.gpsimd, 0, 512, D)
+        load_scales(nc.gpsimd, 0, HEAD_COLS, D)
         load_scales(nc.gpsimd, 1, 0, D)
         nc.gpsimd.dma_start(out=a_bf[:], in_=A_stat)
         nc.gpsimd.dma_start(out=m_bf[:], in_=M_mask)
-        load_words(0)
-        load_words(1)
+        for x, first, n, bank in SETS:
+            for g in range(KG):
+                load_words(x, g, first, n)
+        for g in range(KG - 1):
+            load_words(LAST[0], g, LAST[1], LAST[2])
+        blk = LAST[1]
+        for n in LAST_CUT:
+            load_words(LAST[0], KG - 1, blk, n)
+            blk += n
 
         idle = banks.tile([P, 512], F32, tag="bank7", name="idle")
 
@@ -139,43 +145,56 @@ def tile_dynamicgraphattention_w_kernel(
         x_words = [keep.tile([P, TOK], U32, align_bytes=64, name="x_words%d" % c) for c in range(NCH)]
         x_scale = [keep.tile([P, TOK], U8, align_bytes=64, name="x_scale%d" % c) for c in range(NCH)]
 
-        def passes(x, blk, dst, tok):
-            i, j = where[x][blk]
+        def one_pass(dst, x, blk, g, tok, start, stop):
             col = D * x + P * blk
+            nc.tensor.matmul_mx(
+                out=dst,
+                lhsT=w_sb[(x, g, blk)].bitcast(FP8X4),
+                lhsT_scale=planes[4 * g : P, col : col + P],
+                rhs=h_words[:, g, tok].bitcast(FP8X4),
+                rhs_scale=h_scale[:, g, tok],
+                start=start,
+                stop=stop,
+            )
+
+        def project_set(x, first, n, bank):
+            ps = [
+                banks.tile([P, 2, TOK], F32, tag="bank%d" % (bank + i), name="ps%d_%d" % (x, first + 2 * i))
+                for i in range(n // 2)
+            ]
             for g in range(KG):
-                nc.tensor.matmul_mx(
-                    out=dst,
-                    lhsT=w_sb[x][i][:, g, P * j : P * (j + 1)].bitcast(FP8X4),
-                    lhsT_scale=planes[4 * g : P, col : col + P],
-                    rhs=h_words[:, g, tok].bitcast(FP8X4),
-                    rhs_scale=h_scale[:, g, tok],
-                    start=(g == 0),
-                    stop=(g == KG - 1),
-                )
+                for j in range(n):
+                    one_pass(
+                        ps[j // 2][:, j % 2, :], x, first + j, g, slice(0, TOK),
+                        g == 0 and j % 2 == 0, g == KG - 1 and j % 2 == 1,
+                    )
+            chunks = [DG * x + first // 4 + q for q in range(n // 4)]
+            grouped = [
+                ring.tile([P, 4 * TOK], BF16, align_bytes=64, tag="grouped", name="grouped%d" % c) for c in chunks
+            ]
+            for q in range(n // 4):
+                gview = grouped[q][:].rearrange("p (w t) -> p w t", t=4)
+                for u in range(2):
+                    dst = gview[:, :, 2 * u : 2 * u + 2]
+                    src = ps[2 * q + u][:].rearrange("p e w -> p w e")
+                    if q == 0:
+                        nc.scalar.copy(out=dst, in_=src)
+                    else:
+                        nc.vector.tensor_copy(out=dst, in_=src)
+            for q, c in enumerate(chunks):
+                nc.vector.quantize_mx(out=x_words[c][:].bitcast(FP8X4), scales=x_scale[c][:], in_=grouped[q][:])
 
-        def project(c):
-            x, grp = c // DG, c % DG
-            grouped = ring.tile([P, 4 * TOK], BF16, align_bytes=64, tag="grouped", name="grouped%d" % c)
-            gview = grouped[:].rearrange("p (w t) -> p w t", t=4)
-            for u in range(2):
-                ps = banks.tile([P, 2, TOK], F32, tag="bank%d" % ((4 + 2 * c + u) % 8), name="ps%d_%d" % (c, u))
-                for e in range(2):
-                    passes(x, 4 * grp + 2 * u + e, ps[:, e, :], slice(0, TOK))
-                dst = gview[:, :, 2 * u : 2 * u + 2]
-                src = ps[:].rearrange("p e w -> p w e")
-                if c % 2 == 0:
-                    nc.scalar.copy(out=dst, in_=src)
-                else:
-                    nc.vector.tensor_copy(out=dst, in_=src)
-            nc.vector.quantize_mx(out=x_words[c][:].bitcast(FP8X4), scales=x_scale[c][:], in_=grouped[:])
-
-        def project_last(c):
-            x, grp = c // DG, c % DG
-            ps = [banks.tile([P, 4, P], F32, tag="bank%d" % ((4 + 2 * c + b) % 8), name="pl%d" % b) for b in range(B)]
+        def project_last(x, first, n, bank):
+            c = DG * x + first // 4
+            ps = [banks.tile([P, 4, P], F32, tag="bank%d" % (bank + b), name="pl%d" % b) for b in range(B)]
             grouped = [keep.tile([P, 4 * P], BF16, align_bytes=64, name="glast%d" % b) for b in range(B)]
-            for t in range(4):
-                for b in range(B):
-                    passes(x, 4 * grp + t, ps[b][:, t, :], slice(P * b, P * (b + 1)))
+            for g in range(KG):
+                for t in range(n):
+                    for b in range(B):
+                        one_pass(
+                            ps[b][:, t, :], x, first + t, g, slice(P * b, P * (b + 1)),
+                            g == 0 and t == 0, g == KG - 1 and t == n - 1,
+                        )
             for b in range(B):
                 dst = grouped[b][:].rearrange("p (w t) -> p w t", t=4)
                 src = ps[b][:].rearrange("p t w -> p w t")
@@ -203,11 +222,11 @@ def tile_dynamicgraphattention_w_kernel(
             nc.vector.tensor_scalar(out=neg_b[:], in0=allowed[:], scalar1=-BIG, scalar2=BIG, op0=ALU.mult, op1=ALU.add)
             nc.vector.tensor_tensor(out=neg_b[:], in0=neg_b[:], in1=a_keep[:], op=ALU.subtract)
 
-        for c in range(NCH - 1):
-            project(c)
-            if c == 3:
+        for i, (x, first, n, bank) in enumerate(SETS):
+            project_set(x, first, n, bank)
+            if i == 1:
                 build_mask()
-        project_last(NCH - 1)
+        project_last(LAST[0], LAST[1], LAST[2], LAST[3])
 
         lg = [banks.tile([P, P], F32, tag="bank%d" % (4 + b), name="lg%d" % b) for b in range(B)]
         for grp in range(DG):

@@ -62,8 +62,8 @@ def tile_dynamicgraphattention_w_kernel(
         def load_scales(queue, x, lo, hi):
             for q in range(4):
                 queue.dma_start(
-                    out=planes[32 * q : 32 * q + 16, D * x + lo : D * x + hi].bitcast(F32),
-                    in_=scales[x][:, 4 * q : 4 * q + 4, lo:hi].bitcast(F32),
+                    out=planes[32 * q : 32 * q + 16, D * x + lo : D * x + hi].bitcast(I32),
+                    in_=scales[x][:, 4 * q : 4 * q + 4, lo:hi].bitcast(I32),
                 )
 
         def load_words(x, g, blk, n):
@@ -76,10 +76,9 @@ def tile_dynamicgraphattention_w_kernel(
         h_src = H_t.rearrange("b n c -> n b c")
         for s in range(2):
             nc.sync.dma_start(out=h_sb[s][:], in_=h_src[:, :, (C // 2) * s : (C // 2) * (s + 1)])
-        load_scales(nc.scalar, 0, 0, HEAD_COLS)
+        load_scales(nc.sync, 0, 0, D)
+        load_scales(nc.sync, 1, 0, D)
         nc.scalar.activation(out=warm2[:], in_=warm[:], func=ACT.Exp)
-        load_scales(nc.gpsimd, 0, HEAD_COLS, D)
-        load_scales(nc.gpsimd, 1, 0, D)
         nc.gpsimd.dma_start(out=a_bf[:], in_=A_stat)
         nc.gpsimd.dma_start(out=m_bf[:], in_=M_mask)
         for x, first, n, bank in SETS:

from contextlib import ExitStack
import math

import concourse.mybir as mybir
from concourse.masks import make_identity

F32 = mybir.dt.float32
BF16 = mybir.dt.bfloat16
I32 = mybir.dt.int32
U32 = mybir.dt.uint32
U8 = mybir.dt.uint8
FP8X4 = mybir.dt.float8_e4m3fn_x4
ALU = mybir.AluOpType
ACT = mybir.ActivationFunctionType

P = 128
B = 2
C = 2048
D = 2048
TOK = B * P
KG = C // 512
DG = D // 512
NCH = 2 * DG
TAU = 1.5
BIG = 1.0e30
SETS = ((0, 0, 8, 4), (0, 8, 8, 0), (1, 0, 8, 4), (1, 8, 4, 0))
LAST = (1, 12, 4, 2)
LAST_CUT = (2, 1, 1)
HEAD_COLS = 1024

FLOPS = 2 * 2 * B * P * C * D + 2 * B * P * P * D


def tile_dynamicgraphattention_w_kernel(
    tc, H_t, A_stat, M_mask, Wq_words, Wq_scales, Wk_words, Wk_scales, out
):
    nc = tc.nc
    words = (Wq_words, Wk_words)
    scales = (Wq_scales, Wk_scales)
    with ExitStack() as ctx:
        keep = ctx.enter_context(tc.tile_pool(name="keep", bufs=1))
        ring = ctx.enter_context(tc.tile_pool(name="ring", bufs=4))
        banks = ctx.enter_context(tc.psum_pool(name="banks", bufs=1))
        ctx.enter_context(tc.manual_schedule())

        planes = keep.tile([P, 2 * D], U8, align_bytes=64, name="planes")
        h_sb = [keep.tile([P, B, C // 2], BF16, name="h_sb%d" % s) for s in range(2)]
        w_sb = {}
        zeros = keep.tile([P, 512], BF16, name="zeros")
        a_bf = keep.tile([P, P], BF16, name="a_bf")
        m_bf = keep.tile([P, P], BF16, name="m_bf")
        ident = keep.tile([P, P], F32, name="ident")
        warm = keep.tile([P, 1], F32, name="warm")
        warm2 = keep.tile([P, 1], F32, name="warm2")

        nc.vector.memset(ident[:], 0.0)
        nc.vector.memset(planes[:].bitcast(I32), 0)
        nc.vector.memset(zeros[:].bitcast(I32), 0)
        nc.vector.memset(warm[:], 0.0)
        make_identity(nc, ident[:], nomemset=True)

        def load_scales(queue, x, lo, hi):
            for q in range(4):
                queue.dma_start(
                    out=planes[32 * q : 32 * q + 16, D * x + lo : D * x + hi].bitcast(I32),
                    in_=scales[x][:, 4 * q : 4 * q + 4, lo:hi].bitcast(I32),
                )

        def load_words(x, g, blk, n):
            src = words[x].rearrange("g p n t -> p g (n t)")
            piece = keep.tile([P, P * n], U32, align_bytes=64, name="w_sb%d_%d_%d" % (x, g, blk))
            nc.sync.dma_start(out=piece[:].bitcast(I32), in_=src[:, g, 512 * blk : 512 * (blk + n)].bitcast(I32))
            for j in range(n):
                w_sb[(x, g, blk + j)] = piece[:, P * j : P * (j + 1)]

        h_src = H_t.rearrange("b n c -> n b c")
        for s in range(2):
            nc.sync.dma_start(out=h_sb[s][:], in_=h_src[:, :, (C // 2) * s : (C // 2) * (s + 1)])
        load_scales(nc.sync, 0, 0, D)
        load_scales(nc.sync, 1, 0, D)
        nc.scalar.activation(out=warm2[:], in_=warm[:], func=ACT.Exp)
        nc.gpsimd.dma_start(out=a_bf[:], in_=A_stat)
        nc.gpsimd.dma_start(out=m_bf[:], in_=M_mask)
        for x, first, n, bank in SETS:
            for g in range(KG):
                load_words(x, g, first, n)
        for g in range(KG - 1):
            load_words(LAST[0], g, LAST[1], LAST[2])
        blk = LAST[1]
        for n in LAST_CUT:
            load_words(LAST[0], KG - 1, blk, n)
            blk += n

        idle = banks.tile([P, 512], F32, tag="bank7", name="idle")

        def spin(n):
            for i in range(n):
                nc.tensor.matmul(out=idle[:], lhsT=zeros[:, 0:P], rhs=zeros[:], start=True, stop=True)

        spin(6)

        h_words = keep.tile([P, KG, TOK], U32, align_bytes=64, name="h_words")
        h_scale = keep.tile([P, KG, TOK], U8, align_bytes=64, name="h_scale")
        h_grp = [keep.tile([P, 4 * TOK], BF16, align_bytes=64, name="h_grp%d" % g) for g in range(KG)]
        xt = [banks.tile([P, 2, TOK], F32, tag="bank%d" % g, name="xt%d" % g) for g in range(KG)]

        def h_transposes(g):
            for b in range(B):
                hw32 = h_sb[g // 2][:, b, :].bitcast(F32)
                for u in range(2):
                    nc.tensor.transpose(
                        xt[g][:, u, P * b : P * (b + 1)],
                        hw32[:, 256 * (g % 2) + u : 256 * (g % 2 + 1) : 2],
                        ident[:],
                    )

        def h_copy(g):
            dst = h_grp[g][:].bitcast(F32).rearrange("p (w u) -> p w u", u=2)
            src = xt[g][:].rearrange("p u w -> p w u")
            if g % 2 == 0:
                nc.vector.tensor_copy(out=dst, in_=src)
            else:
                nc.scalar.copy(out=dst, in_=src)

        def h_quantise(g):
            nc.vector.quantize_mx(
                out=h_words[:, g, :].bitcast(FP8X4), scales=h_scale[:, g, :], in_=h_grp[g][:]
            )

        h_transposes(0)
        h_transposes(1)
        spin(1)
        h_transposes(2)
        h_transposes(3)
        h_copy(0)
        h_copy(1)
        h_quantise(0)
        h_copy(2)
        h_copy(3)
        h_quantise(1)
        h_quantise(2)
        h_quantise(3)

        x_words = [keep.tile([P, TOK], U32, align_bytes=64, name="x_words%d" % c) for c in range(NCH)]
        x_scale = [keep.tile([P, TOK], U8, align_bytes=64, name="x_scale%d" % c) for c in range(NCH)]

        def one_pass(dst, x, blk, g, tok, start, stop):
            col = D * x + P * blk
            nc.tensor.matmul_mx(
                out=dst,
                lhsT=w_sb[(x, g, blk)].bitcast(FP8X4),
                lhsT_scale=planes[4 * g : P, col : col + P],
                rhs=h_words[:, g, tok].bitcast(FP8X4),
                rhs_scale=h_scale[:, g, tok],
                start=start,
                stop=stop,
            )

        def project_set(x, first, n, bank):
            ps = [
                banks.tile([P, 2, TOK], F32, tag="bank%d" % (bank + i), name="ps%d_%d" % (x, first + 2 * i))
                for i in range(n // 2)
            ]
            for g in range(KG):
                for j in range(n):
                    one_pass(
                        ps[j // 2][:, j % 2, :], x, first + j, g, slice(0, TOK),
                        g == 0 and j % 2 == 0, g == KG - 1 and j % 2 == 1,
                    )
            chunks = [DG * x + first // 4 + q for q in range(n // 4)]
            grouped = [
                ring.tile([P, 4 * TOK], BF16, align_bytes=64, tag="grouped", name="grouped%d" % c) for c in chunks
            ]
            for q in range(n // 4):
                gview = grouped[q][:].rearrange("p (w t) -> p w t", t=4)
                for u in range(2):
                    dst = gview[:, :, 2 * u : 2 * u + 2]
                    src = ps[2 * q + u][:].rearrange("p e w -> p w e")
                    if q == 0:
                        nc.scalar.copy(out=dst, in_=src)
                    else:
                        nc.vector.tensor_copy(out=dst, in_=src)
            for q, c in enumerate(chunks):
                nc.vector.quantize_mx(out=x_words[c][:].bitcast(FP8X4), scales=x_scale[c][:], in_=grouped[q][:])

        def project_last(x, first, n, bank):
            c = DG * x + first // 4
            ps = [banks.tile([P, 4, P], F32, tag="bank%d" % (bank + b), name="pl%d" % b) for b in range(B)]
            grouped = [keep.tile([P, 4 * P], BF16, align_bytes=64, name="glast%d" % b) for b in range(B)]
            for g in range(KG):
                for t in range(n):
                    for b in range(B):
                        one_pass(
                            ps[b][:, t, :], x, first + t, g, slice(P * b, P * (b + 1)),
                            g == 0 and t == 0, g == KG - 1 and t == n - 1,
                        )
            for b in range(B):
                dst = grouped[b][:].rearrange("p (w t) -> p w t", t=4)
                src = ps[b][:].rearrange("p t w -> p w t")
                if b == 0:
                    nc.scalar.copy(out=dst, in_=src)
                else:
                    nc.vector.tensor_copy(out=dst, in_=src)
            for b in range(B):
                cols = slice(P * b, P * (b + 1))
                nc.vector.quantize_mx(
                    out=x_words[c][:, cols].bitcast(FP8X4), scales=x_scale[c][:, cols], in_=grouped[b][:]
                )

        not_i = keep.tile([P, P], F32, name="not_i")
        allowed = keep.tile([P, P], F32, name="allowed")
        a_keep = keep.tile([P, P], F32, name="a_keep")
        neg_b = keep.tile([P, P], F32, name="neg_b")

        def build_mask():
            nc.vector.tensor_scalar(out=not_i[:], in0=ident[:], scalar1=-1.0, scalar2=1.0, op0=ALU.mult, op1=ALU.add)
            nc.vector.scalar_tensor_tensor(
                out=allowed[:], in0=m_bf[:], scalar=0.0, in1=not_i[:], op0=ALU.is_gt, op1=ALU.mult
            )
            nc.vector.tensor_tensor(out=a_keep[:], in0=a_bf[:], in1=allowed[:], op=ALU.mult)
            nc.vector.tensor_scalar(out=neg_b[:], in0=allowed[:], scalar1=-BIG, scalar2=BIG, op0=ALU.mult, op1=ALU.add)
            nc.vector.tensor_tensor(out=neg_b[:], in0=neg_b[:], in1=a_keep[:], op=ALU.subtract)

        for i, (x, first, n, bank) in enumerate(SETS):
            project_set(x, first, n, bank)
            if i == 1:
                build_mask()
        project_last(LAST[0], LAST[1], LAST[2], LAST[3])

        lg = [banks.tile([P, P], F32, tag="bank%d" % (4 + b), name="lg%d" % b) for b in range(B)]
        for grp in range(DG):
            cq, ck = grp, DG + grp
            for b in range(B):
                cols = slice(P * b, P * (b + 1))
                for second, (l, r) in enumerate(((cq, ck), (ck, cq))):
                    nc.tensor.matmul_mx(
                        out=lg[b][:],
                        lhsT=x_words[l][:, cols].bitcast(FP8X4),
                        lhsT_scale=x_scale[l][:, cols],
                        rhs=x_words[r][:, cols].bitcast(FP8X4),
                        rhs_scale=x_scale[r][:, cols],
                        start=(grp == 0 and second == 0),
                        stop=(grp == DG - 1 and second == 1),
                    )

        y = keep.tile([P, B, P], F32, name="y")
        ex = keep.tile([P, B, P], F32, name="ex")
        res = keep.tile([P, B, P], F32, name="res")
        nmax = keep.tile([P, B], F32, name="nmax")
        ssum = keep.tile([P, B], F32, name="ssum")
        rsum = keep.tile([P, B], F32, name="rsum")
        cneg = -0.5 / (math.sqrt(C) * TAU)
        for b in range(B):
            nc.vector.scalar_tensor_tensor(
                out=y[:, b, :], in0=lg[b][:], scalar=cneg, in1=neg_b[:], op0=ALU.mult, op1=ALU.add
            )
            nc.vector.tensor_reduce(out=nmax[:, b : b + 1], in_=y[:, b, :], axis=mybir.AxisListType.X, op=ALU.min)
            nc.scalar.activation(
                out=ex[:, b, :], in_=y[:, b, :], func=ACT.Exp, bias=nmax[:, b : b + 1], scale=-1.0,
                accum_out=ssum[:, b : b + 1],
            )
        for b in range(B):
            nc.vector.reciprocal(out=rsum[:, b : b + 1], in_=ssum[:, b : b + 1])
            nc.vector.tensor_scalar(
                out=res[:, b, :], in0=ex[:, b, :], scalar1=rsum[:, b : b + 1], scalar2=None, op0=ALU.mult
            )
            nc.sync.dma_start(out=out[b], in_=res[:, b, :])
